import numpy as np
import ml_dtypes

BF16 = ml_dtypes.bfloat16


def bf(x):
    return np.asarray(x, np.float32).astype(BF16)


def f32(x):
    return np.asarray(x, np.float32)


def f64(x):
    return np.asarray(x).astype(np.float64)


def striped(idx):
    return np.tile(idx.reshape(-1, 16).T, (8, 1))


C, F, S, N = 256, 1024, 4096, 2048
EPS = 1e-5


def erf(a):
    a = np.asarray(a, np.float64)
    t = np.clip(a, -6.0, 6.0)
    term = t.copy()
    tot = t.copy()
    for n in range(1, 150):
        term = term * 2.0 * t * t / (2.0 * n + 1.0)
        tot = tot + term
    r = 2.0 / np.sqrt(np.pi) * np.exp(-t * t) * tot
    return np.where(np.abs(a) > 6.0, np.sign(a), r)


def gelu_erf(v):
    return 0.5 * v * (1.0 + erf(v / np.sqrt(2.0)))


def setup_inputs():
    return {"base": f32(np.random.standard_normal((C, S))), "x": f32(np.random.standard_normal((C, N))), "ln_gain": f32(1.0 + 0.1 * np.random.standard_normal((C, 1))), "ln_bias": f32(0.1 * np.random.standard_normal((C, 1))), "w1": bf(np.random.standard_normal((C, F)) / np.sqrt(C)), "b1": f32(0.1 * np.random.standard_normal((F, 1))), "w2": bf(np.random.standard_normal((F, C)) / np.sqrt(F)), "b2": f32(0.1 * np.random.standard_normal((C, 1))), "offs": striped(np.random.permutation(S)[:N])}


def reference(base, x, ln_gain, ln_bias, w1, b1, w2, b2, offs):
    idx = offs[:16].T.reshape(-1)
    xv = f64(x)
    mu = xv.mean(axis=0, keepdims=True)
    var = np.square(xv - mu).mean(axis=0, keepdims=True)
    nrm = (xv - mu) / np.sqrt(var + EPS) * f64(ln_gain) + f64(ln_bias)
    h = gelu_erf(f64(w1).T @ nrm + f64(b1))
    mlp = f64(w2).T @ h + f64(b2)
    out = f64(base).copy()
    out[:, idx] = xv + mlp
    return out

@@ -1,0 +1,135 @@
+import concourse.mybir as mybir
+from concourse.masks import make_identity
+
+F32 = mybir.dt.float32
+BF16 = mybir.dt.bfloat16
+U16 = mybir.dt.uint16
+ALU = mybir.AluOpType
+ACT = mybir.ActivationFunctionType
+
+P = 128
+C, F, S, N = 256, 1024, 4096, 2048
+CB = C // P
+FB = F // P
+TOK = 512
+NCH = N // TOK
+EPS = 1e-5
+
+GAIN, BIAS, B2, B1 = 0, CB, 2 * CB, 3 * CB
+NVEC = 3 * CB + FB
+
+FLOPS = 2 * N * C * F * 2
+
+
+def tile_stoichiometricmab_kernel(tc, base, x, ln_gain, ln_bias, w1, b1, w2, b2, offs, out):
+    nc = tc.nc
+    with (
+        tc.tile_pool(name="held", bufs=1) as held,
+        tc.psum_pool(name="psum", bufs=8) as psum,
+    ):
+        x_sb = held.tile([P, CB, N], F32, name="x_sb")
+        x_blocks = x.rearrange("(cb p) n -> p cb n", p=P)
+        for n in range(NCH):
+            queue = nc.sync if n % 2 == 0 else nc.scalar
+            queue.dma_start(x_sb[:, :, n * TOK : (n + 1) * TOK], x_blocks[:, :, n * TOK : (n + 1) * TOK])
+
+        rows = held.tile([P, P], F32, name="rows")
+        nc.vector.memset(rows[:], 0.0)
+        for vector, first, blocks in ((ln_gain, GAIN, CB), (ln_bias, BIAS, CB), (b2, B2, CB), (b1, B1, FB)):
+            nc.gpsimd.dma_start(rows[first : first + blocks, :], vector.rearrange("(r p) o -> r (p o)", p=P))
+
+        w1_sb = held.tile([P, CB, F], BF16, name="w1_sb")
+        nc.sync.dma_start(w1_sb[:], w1.rearrange("(cb p) f -> p cb f", p=P))
+        w2_sb = held.tile([P, FB, C], BF16, name="w2_sb")
+        nc.scalar.dma_start(w2_sb[:], w2.rearrange("(fb p) c -> p fb c", p=P))
+
+        offsets = held.tile([P, N // 16], U16, name="offsets")
+        nc.sync.dma_start(offsets[:], offs)
+
+        window = [held.tile([P, S], F32, name=f"window{cb}") for cb in range(CB)]
+        nc.sync.dma_start(window[0][:], base[0:P, :])
+        nc.scalar.dma_start(window[1][:], base[P : 2 * P, :])
+
+        averager = held.tile([P, P], F32, name="averager")
+        nc.vector.memset(averager[:], 1.0 / C)
+        eps_col = held.tile([P, 1], F32, name="eps_col")
+        nc.vector.memset(eps_col[:], EPS)
+        ident = held.tile([P, P], F32, name="ident")
+        make_identity(nc, ident[:])
+
+        cols_ps = psum.tile([P, TOK], F32, name="cols_ps", tag="bank")
+        nc.tensor.transpose(cols_ps[:, 0:P], rows[:], ident[:])
+        cols = held.tile([P, NVEC], F32, name="cols")
+        nc.vector.tensor_copy(cols[:], cols_ps[:, 0:NVEC])
+
+        centered = held.tile([P, CB, N], F32, name="centered")
+        squared = held.tile([P, CB, N], F32, name="squared")
+        rstd = held.tile([P, N], F32, name="rstd")
+        nrm = held.tile([P, CB, N], BF16, name="nrm")
+
+        for n in range(NCH):
+            chunk = slice(n * TOK, (n + 1) * TOK)
+            mean_ps = psum.tile([P, TOK], F32, name="mean_ps", tag="bank")
+            for cb in range(CB):
+                nc.tensor.matmul(mean_ps[:], averager[:], x_sb[:, cb, chunk], start=(cb == 0), stop=(cb == CB - 1))
+            mean_both = mean_ps[:].unsqueeze(1).to_broadcast([P, CB, TOK])
+            nc.vector.tensor_tensor(centered[:, :, chunk], x_sb[:, :, chunk], mean_both, ALU.subtract)
+            nc.scalar.activation(squared[:, :, chunk], centered[:, :, chunk], ACT.Square)
+
+        for n in range(NCH):
+            chunk = slice(n * TOK, (n + 1) * TOK)
+            var_ps = psum.tile([P, TOK], F32, name="var_ps", tag="bank")
+            for cb in range(CB):
+                nc.tensor.matmul(var_ps[:], averager[:], squared[:, cb, chunk], start=(cb == 0), stop=(cb == CB - 1))
+            nc.scalar.activation(rstd[:, chunk], var_ps[:], ACT.Abs_reciprocal_sqrt, bias=eps_col[:])
+            rstd_both = rstd[:, chunk].unsqueeze(1).to_broadcast([P, CB, TOK])
+            nc.vector.tensor_tensor(centered[:, :, chunk], centered[:, :, chunk], rstd_both, ALU.mult)
+            for cb in range(CB):
+                nc.vector.tensor_scalar(
+                    nrm[:, cb, chunk],
+                    centered[:, cb, chunk],
+                    cols[:, GAIN + cb : GAIN + cb + 1],
+                    cols[:, BIAS + cb : BIAS + cb + 1],
+                    ALU.mult,
+                    ALU.add,
+                )
+
+        hidden = held.tile([P, FB, N], BF16, name="hidden")
+        mlp = [held.tile([P, N], F32, name=f"mlp{cb}") for cb in range(CB)]
+
+        def first_matmul(n):
+            chunk = slice(n * TOK, (n + 1) * TOK)
+            for fb in range(FB):
+                h_ps = psum.tile([P, TOK], F32, name="h_ps", tag="bank")
+                for cb in range(CB):
+                    nc.tensor.matmul(
+                        h_ps[:], w1_sb[:, cb, fb * P : (fb + 1) * P], nrm[:, cb, chunk], start=(cb == 0), stop=(cb == CB - 1)
+                    )
+                nc.scalar.activation(hidden[:, fb, chunk], h_ps[:], ACT.Gelu, bias=cols[:, B1 + fb : B1 + fb + 1])
+
+        def second_matmul(n, cb):
+            chunk = slice(n * TOK, (n + 1) * TOK)
+            mlp_ps = psum.tile([P, TOK], F32, name="mlp_ps", tag="bank")
+            for fb in range(FB):
+                nc.tensor.matmul(
+                    mlp_ps[:], w2_sb[:, fb, cb * P : (cb + 1) * P], hidden[:, fb, chunk], start=(fb == 0), stop=(fb == FB - 1)
+                )
+            b2_col = cols[:, B2 + cb : B2 + cb + 1]
+            if cb == 0:
+                nc.vector.tensor_scalar_add(mlp[cb][:, chunk], mlp_ps[:], b2_col)
+            else:
+                nc.scalar.activation(mlp[cb][:, chunk], mlp_ps[:], ACT.Identity, bias=b2_col)
+
+        def place(cb):
+            nc.vector.tensor_tensor(window[cb][:].indirect(offsets[:]), mlp[cb][:], x_sb[:, cb, :], ALU.add)
+            nc.sync.dma_start(out[cb * P : (cb + 1) * P, :], window[cb][:])
+
+        first_matmul(0)
+        for n in range(1, NCH):
+            first_matmul(n)
+            second_matmul(n - 1, 0)
+        second_matmul(NCH - 1, 0)
+        place(0)
+        for n in range(NCH):
+            second_matmul(n, 1)
+        place(1)

@@ -36,7 +36,7 @@ def tile_stoichiometricmab_kernel(tc, base, x, ln_gain, ln_bias, w1, b1, w2, b2,
         rows = held.tile([P, P], F32, name="rows")
         nc.vector.memset(rows[:], 0.0)
         for vector, first, blocks in ((ln_gain, GAIN, CB), (ln_bias, BIAS, CB), (b2, B2, CB), (b1, B1, FB)):
-            nc.gpsimd.dma_start(rows[first : first + blocks, :], vector.rearrange("(r p) o -> r (p o)", p=P))
+            nc.scalar.dma_start(rows[first : first + blocks, :], vector.rearrange("(r p) o -> r (p o)", p=P))
 
         w1_sb = held.tile([P, CB, F], BF16, name="w1_sb")
         nc.sync.dma_start(w1_sb[:], w1.rearrange("(cb p) f -> p cb f", p=P))
@@ -57,11 +57,6 @@ def tile_stoichiometricmab_kernel(tc, base, x, ln_gain, ln_bias, w1, b1, w2, b2,
         ident = held.tile([P, P], F32, name="ident")
         make_identity(nc, ident[:])
 
-        cols_ps = psum.tile([P, TOK], F32, name="cols_ps", tag="bank")
-        nc.tensor.transpose(cols_ps[:, 0:P], rows[:], ident[:])
-        cols = held.tile([P, NVEC], F32, name="cols")
-        nc.vector.tensor_copy(cols[:], cols_ps[:, 0:NVEC])
-
         centered = held.tile([P, CB, N], F32, name="centered")
         squared = held.tile([P, CB, N], F32, name="squared")
         rstd = held.tile([P, N], F32, name="rstd")
@@ -75,6 +70,11 @@ def tile_stoichiometricmab_kernel(tc, base, x, ln_gain, ln_bias, w1, b1, w2, b2,
             mean_both = mean_ps[:].unsqueeze(1).to_broadcast([P, CB, TOK])
             nc.vector.tensor_tensor(centered[:, :, chunk], x_sb[:, :, chunk], mean_both, ALU.subtract)
             nc.scalar.activation(squared[:, :, chunk], centered[:, :, chunk], ACT.Square)
+
+        cols_ps = psum.tile([P, TOK], F32, name="cols_ps", tag="bank")
+        nc.tensor.transpose(cols_ps[:, 0:P], rows[:], ident[:])
+        cols = held.tile([P, NVEC], F32, name="cols")
+        nc.vector.tensor_copy(cols[:], cols_ps[:, 0:NVEC])
 
         for n in range(NCH):
             chunk = slice(n * TOK, (n + 1) * TOK)

@@ -10,6 +10,7 @@ ACT = mybir.ActivationFunctionType
 P = 128
 C, F, S, N = 256, 1024, 4096, 2048
 CB = C // P
+assert CB == 2
 FB = F // P
 TOK = 512
 NCH = N // TOK
@@ -57,16 +58,18 @@ def tile_stoichiometricmab_kernel(tc, base, x, ln_gain, ln_bias, w1, b1, w2, b2,
         ident = held.tile([P, P], F32, name="ident")
         make_identity(nc, ident[:])
 
+        x_sum = held.tile([P, N], F32, name="x_sum")
         centered = held.tile([P, CB, N], F32, name="centered")
         squared = held.tile([P, CB, N], F32, name="squared")
+        squared_sum = held.tile([P, N], F32, name="squared_sum")
         rstd = held.tile([P, N], F32, name="rstd")
         nrm = held.tile([P, CB, N], BF16, name="nrm")
 
         for n in range(NCH):
             chunk = slice(n * TOK, (n + 1) * TOK)
+            nc.gpsimd.tensor_tensor(x_sum[:, chunk], x_sb[:, 0, chunk], x_sb[:, 1, chunk], ALU.add)
             mean_ps = psum.tile([P, TOK], F32, name="mean_ps", tag="bank")
-            for cb in range(CB):
-                nc.tensor.matmul(mean_ps[:], averager[:], x_sb[:, cb, chunk], start=(cb == 0), stop=(cb == CB - 1))
+            nc.tensor.matmul(mean_ps[:], averager[:], x_sum[:, chunk], start=True, stop=True)
             mean_both = mean_ps[:].unsqueeze(1).to_broadcast([P, CB, TOK])
             nc.vector.tensor_tensor(centered[:, :, chunk], x_sb[:, :, chunk], mean_both, ALU.subtract)
             nc.scalar.activation(squared[:, :, chunk], centered[:, :, chunk], ACT.Square)
@@ -78,9 +81,9 @@ def tile_stoichiometricmab_kernel(tc, base, x, ln_gain, ln_bias, w1, b1, w2, b2,
 
         for n in range(NCH):
             chunk = slice(n * TOK, (n + 1) * TOK)
+            nc.gpsimd.tensor_tensor(squared_sum[:, chunk], squared[:, 0, chunk], squared[:, 1, chunk], ALU.add)
             var_ps = psum.tile([P, TOK], F32, name="var_ps", tag="bank")
-            for cb in range(CB):
-                nc.tensor.matmul(var_ps[:], averager[:], squared[:, cb, chunk], start=(cb == 0), stop=(cb == CB - 1))
+            nc.tensor.matmul(var_ps[:], averager[:], squared_sum[:, chunk], start=True, stop=True)
             nc.scalar.activation(rstd[:, chunk], var_ps[:], ACT.Abs_reciprocal_sqrt, bias=eps_col[:])
             rstd_both = rstd[:, chunk].unsqueeze(1).to_broadcast([P, CB, TOK])
             nc.vector.tensor_tensor(centered[:, :, chunk], centered[:, :, chunk], rstd_both, ALU.mult)

@@ -29,27 +29,27 @@ def tile_stoichiometricmab_kernel(tc, base, x, ln_gain, ln_bias, w1, b1, w2, b2,
         tc.psum_pool(name="psum", bufs=8) as psum,
     ):
         x_sb = held.tile([P, CB, N], F32, name="x_sb")
-        x_blocks = x.rearrange("(cb p) n -> p cb n", p=P)
         for n in range(NCH):
-            queue = nc.sync if n % 2 == 0 else nc.scalar
-            queue.dma_start(x_sb[:, :, n * TOK : (n + 1) * TOK], x_blocks[:, :, n * TOK : (n + 1) * TOK])
+            chunk = slice(n * TOK, (n + 1) * TOK)
+            nc.sync.dma_start(x_sb[:, 0, chunk], x[0:P, chunk])
+            nc.scalar.dma_start(x_sb[:, 1, chunk], x[P : 2 * P, chunk])
 
         rows = held.tile([P, P], F32, name="rows")
         nc.vector.memset(rows[:], 0.0)
         for vector, first, blocks in ((ln_gain, GAIN, CB), (ln_bias, BIAS, CB), (b2, B2, CB), (b1, B1, FB)):
-            nc.scalar.dma_start(rows[first : first + blocks, :], vector.rearrange("(r p) o -> r (p o)", p=P))
+            nc.sync.dma_start(rows[first : first + blocks, :], vector.rearrange("(r p) o -> r (p o)", p=P))
 
         w1_sb = held.tile([P, CB, F], BF16, name="w1_sb")
         nc.sync.dma_start(w1_sb[:], w1.rearrange("(cb p) f -> p cb f", p=P))
         w2_sb = held.tile([P, FB, C], BF16, name="w2_sb")
-        nc.scalar.dma_start(w2_sb[:], w2.rearrange("(fb p) c -> p fb c", p=P))
+        nc.sync.dma_start(w2_sb[:], w2.rearrange("(fb p) c -> p fb c", p=P))
 
         offsets = held.tile([P, N // 16], U16, name="offsets")
         nc.sync.dma_start(offsets[:], offs)
 
         window = [held.tile([P, S], F32, name=f"window{cb}") for cb in range(CB)]
-        nc.sync.dma_start(window[0][:], base[0:P, :])
-        nc.scalar.dma_start(window[1][:], base[P : 2 * P, :])
+        for cb in range(CB):
+            nc.sync.dma_start(window[cb][:], base[cb * P : (cb + 1) * P, :])
 
         averager = held.tile([P, P], F32, name="averager")
         nc.vector.memset(averager[:], 1.0 / C)
@@ -67,7 +67,10 @@ def tile_stoichiometricmab_kernel(tc, base, x, ln_gain, ln_bias, w1, b1, w2, b2,
 
         for n in range(NCH):
             chunk = slice(n * TOK, (n + 1) * TOK)
-            nc.gpsimd.tensor_tensor(x_sum[:, chunk], x_sb[:, 0, chunk], x_sb[:, 1, chunk], ALU.add)
+            nc.vector.tensor_tensor(x_sum[:, chunk], x_sb[:, 0, chunk], x_sb[:, 1, chunk], ALU.add)
+
+        for n in range(NCH):
+            chunk = slice(n * TOK, (n + 1) * TOK)
             mean_ps = psum.tile([P, TOK], F32, name="mean_ps", tag="bank")
             nc.tensor.matmul(mean_ps[:], averager[:], x_sum[:, chunk], start=True, stop=True)
             mean_both = mean_ps[:].unsqueeze(1).to_broadcast([P, CB, TOK])

@@ -14,6 +14,8 @@ assert CB == 2
 FB = F // P
 TOK = 512
 NCH = N // TOK
+LNW = 256
+NLN = N // LNW
 EPS = 1e-5
 
 GAIN, BIAS, B2, B1 = 0, CB, 2 * CB, 3 * CB
@@ -65,35 +67,35 @@ def tile_stoichiometricmab_kernel(tc, base, x, ln_gain, ln_bias, w1, b1, w2, b2,
         rstd = held.tile([P, N], F32, name="rstd")
         nrm = held.tile([P, CB, N], BF16, name="nrm")
 
-        for n in range(NCH):
-            chunk = slice(n * TOK, (n + 1) * TOK)
-            nc.vector.tensor_tensor(x_sum[:, chunk], x_sb[:, 0, chunk], x_sb[:, 1, chunk], ALU.add)
+        for i in range(NLN):
+            piece = slice(i * LNW, (i + 1) * LNW)
+            nc.vector.tensor_tensor(x_sum[:, piece], x_sb[:, 0, piece], x_sb[:, 1, piece], ALU.add)
 
-        for n in range(NCH):
-            chunk = slice(n * TOK, (n + 1) * TOK)
+        for i in range(NLN):
+            piece = slice(i * LNW, (i + 1) * LNW)
             mean_ps = psum.tile([P, TOK], F32, name="mean_ps", tag="bank")
-            nc.tensor.matmul(mean_ps[:], averager[:], x_sum[:, chunk], start=True, stop=True)
-            mean_both = mean_ps[:].unsqueeze(1).to_broadcast([P, CB, TOK])
-            nc.vector.tensor_tensor(centered[:, :, chunk], x_sb[:, :, chunk], mean_both, ALU.subtract)
-            nc.scalar.activation(squared[:, :, chunk], centered[:, :, chunk], ACT.Square)
+            nc.tensor.matmul(mean_ps[:, 0:LNW], averager[:], x_sum[:, piece], start=True, stop=True)
+            mean_both = mean_ps[:, 0:LNW].unsqueeze(1).to_broadcast([P, CB, LNW])
+            nc.vector.tensor_tensor(centered[:, :, piece], x_sb[:, :, piece], mean_both, ALU.subtract)
+            nc.scalar.activation(squared[:, :, piece], centered[:, :, piece], ACT.Square)
 
         cols_ps = psum.tile([P, TOK], F32, name="cols_ps", tag="bank")
         nc.tensor.transpose(cols_ps[:, 0:P], rows[:], ident[:])
         cols = held.tile([P, NVEC], F32, name="cols")
         nc.vector.tensor_copy(cols[:], cols_ps[:, 0:NVEC])
 
-        for n in range(NCH):
-            chunk = slice(n * TOK, (n + 1) * TOK)
-            nc.gpsimd.tensor_tensor(squared_sum[:, chunk], squared[:, 0, chunk], squared[:, 1, chunk], ALU.add)
+        for i in range(NLN):
+            piece = slice(i * LNW, (i + 1) * LNW)
+            nc.gpsimd.tensor_tensor(squared_sum[:, piece], squared[:, 0, piece], squared[:, 1, piece], ALU.add)
             var_ps = psum.tile([P, TOK], F32, name="var_ps", tag="bank")
-            nc.tensor.matmul(var_ps[:], averager[:], squared_sum[:, chunk], start=True, stop=True)
-            nc.scalar.activation(rstd[:, chunk], var_ps[:], ACT.Abs_reciprocal_sqrt, bias=eps_col[:])
-            rstd_both = rstd[:, chunk].unsqueeze(1).to_broadcast([P, CB, TOK])
-            nc.vector.tensor_tensor(centered[:, :, chunk], centered[:, :, chunk], rstd_both, ALU.mult)
+            nc.tensor.matmul(var_ps[:, 0:LNW], averager[:], squared_sum[:, piece], start=True, stop=True)
+            nc.scalar.activation(rstd[:, piece], var_ps[:, 0:LNW], ACT.Abs_reciprocal_sqrt, bias=eps_col[:])
+            rstd_both = rstd[:, piece].unsqueeze(1).to_broadcast([P, CB, LNW])
+            nc.vector.tensor_tensor(centered[:, :, piece], centered[:, :, piece], rstd_both, ALU.mult)
             for cb in range(CB):
                 nc.vector.tensor_scalar(
-                    nrm[:, cb, chunk],
-                    centered[:, cb, chunk],
+                    nrm[:, cb, piece],
+                    centered[:, cb, piece],
                     cols[:, GAIN + cb : GAIN + cb + 1],
                     cols[:, BIAS + cb : BIAS + cb + 1],
                     ALU.mult,

@@ -10,16 +10,14 @@ ACT = mybir.ActivationFunctionType
 P = 128
 C, F, S, N = 256, 1024, 4096, 2048
 CB = C // P
-assert CB == 2
 FB = F // P
 TOK = 512
 NCH = N // TOK
-LNW = 256
-NLN = N // LNW
+NT = N // P
+PAIR = TOK // C
+LNW = PAIR * P
+PIECES = TOK // LNW
 EPS = 1e-5
-
-GAIN, BIAS, B2, B1 = 0, CB, 2 * CB, 3 * CB
-NVEC = 3 * CB + FB
 
 FLOPS = 2 * N * C * F * 2
 
@@ -30,21 +28,35 @@ def tile_stoichiometricmab_kernel(tc, base, x, ln_gain, ln_bias, w1, b1, w2, b2,
         tc.tile_pool(name="held", bufs=1) as held,
         tc.psum_pool(name="psum", bufs=8) as psum,
     ):
+        ident = held.tile([P, P], F32, name="ident")
+        make_identity(nc, ident[:])
+        minus_half = held.tile([P, PAIR], F32, name="minus_half")
+        nc.vector.memset(minus_half[:], -0.5)
+
         x_sb = held.tile([P, CB, N], F32, name="x_sb")
-        for n in range(NCH):
+
+        def load_x(n):
             chunk = slice(n * TOK, (n + 1) * TOK)
             nc.sync.dma_start(x_sb[:, 0, chunk], x[0:P, chunk])
             nc.scalar.dma_start(x_sb[:, 1, chunk], x[P : 2 * P, chunk])
 
-        rows = held.tile([P, P], F32, name="rows")
-        nc.vector.memset(rows[:], 0.0)
-        for vector, first, blocks in ((ln_gain, GAIN, CB), (ln_bias, BIAS, CB), (b2, B2, CB), (b1, B1, FB)):
-            nc.sync.dma_start(rows[first : first + blocks, :], vector.rearrange("(r p) o -> r (p o)", p=P))
+        def load_columns(vector, blocks, name):
+            columns = held.tile([P, blocks], F32, name=name)
+            nc.sync.dma_start(columns[:], vector.rearrange("(r p) o -> p (r o)", p=P))
+            return columns
 
+        load_x(0)
+        load_x(1)
+        gain_col = load_columns(ln_gain, CB, "gain_col")
+        bias_col = load_columns(ln_bias, CB, "bias_col")
         w1_sb = held.tile([P, CB, F], BF16, name="w1_sb")
         nc.sync.dma_start(w1_sb[:], w1.rearrange("(cb p) f -> p cb f", p=P))
+        b1_col = load_columns(b1, FB, "b1_col")
+        load_x(2)
+        load_x(3)
         w2_sb = held.tile([P, FB, C], BF16, name="w2_sb")
         nc.sync.dma_start(w2_sb[:], w2.rearrange("(fb p) c -> p fb c", p=P))
+        b2_col = load_columns(b2, CB, "b2_col")
 
         offsets = held.tile([P, N // 16], U16, name="offsets")
         nc.sync.dma_start(offsets[:], offs)
@@ -53,54 +65,62 @@ def tile_stoichiometricmab_kernel(tc, base, x, ln_gain, ln_bias, w1, b1, w2, b2,
         for cb in range(CB):
             nc.sync.dma_start(window[cb][:], base[cb * P : (cb + 1) * P, :])
 
-        averager = held.tile([P, P], F32, name="averager")
-        nc.vector.memset(averager[:], 1.0 / C)
-        eps_col = held.tile([P, 1], F32, name="eps_col")
-        nc.vector.memset(eps_col[:], EPS)
-        ident = held.tile([P, P], F32, name="ident")
-        make_identity(nc, ident[:])
-
-        x_sum = held.tile([P, N], F32, name="x_sum")
-        centered = held.tile([P, CB, N], F32, name="centered")
-        squared = held.tile([P, CB, N], F32, name="squared")
-        squared_sum = held.tile([P, N], F32, name="squared_sum")
-        rstd = held.tile([P, N], F32, name="rstd")
+        stats = held.tile([P, NT, 6], F32, name="stats")
+        mean_var = held.tile([P, NT, 2], F32, name="mean_var")
+        var_eps = held.tile([P, NT], F32, name="var_eps")
+        rstd = held.tile([P, NT], F32, name="rstd")
+        x_hat = held.tile([P, NT, C], F32, name="x_hat")
         nrm = held.tile([P, CB, N], BF16, name="nrm")
+        x_turned = {}
 
-        for i in range(NLN):
-            piece = slice(i * LNW, (i + 1) * LNW)
-            nc.vector.tensor_tensor(x_sum[:, piece], x_sb[:, 0, piece], x_sb[:, 1, piece], ALU.add)
+        def layer_norm_front(n):
+            pieces = range(n * PIECES, (n + 1) * PIECES)
+            for i in pieces:
+                x_turned[i] = psum.tile([P, TOK], F32, name="x_turned", tag="bank")
+                for k in range(PAIR):
+                    tokens = slice((i * PAIR + k) * P, (i * PAIR + k + 1) * P)
+                    for cb in range(CB):
+                        channels = slice(k * C + cb * P, k * C + (cb + 1) * P)
+                        nc.tensor.transpose(x_turned[i][:, channels], x_sb[:, cb, tokens], ident[:])
+            for i in pieces:
+                for k in range(PAIR):
+                    t = i * PAIR + k
+                    nc.vector.bn_stats(stats[:, t, :], x_turned[i][:, k * C : (k + 1) * C])
+                    nc.vector.bn_aggr(mean_var[:, t, :], stats[:, t, :])
+                pair = slice(i * PAIR, (i + 1) * PAIR)
+                nc.gpsimd.tensor_scalar_add(var_eps[:, pair], mean_var[:, pair, 1], EPS)
+                nc.gpsimd.tensor_tensor(rstd[:, pair], var_eps[:, pair], minus_half[:], ALU.pow)
 
-        for i in range(NLN):
-            piece = slice(i * LNW, (i + 1) * LNW)
-            mean_ps = psum.tile([P, TOK], F32, name="mean_ps", tag="bank")
-            nc.tensor.matmul(mean_ps[:, 0:LNW], averager[:], x_sum[:, piece], start=True, stop=True)
-            mean_both = mean_ps[:, 0:LNW].unsqueeze(1).to_broadcast([P, CB, LNW])
-            nc.vector.tensor_tensor(centered[:, :, piece], x_sb[:, :, piece], mean_both, ALU.subtract)
-            nc.scalar.activation(squared[:, :, piece], centered[:, :, piece], ACT.Square)
-
-        cols_ps = psum.tile([P, TOK], F32, name="cols_ps", tag="bank")
-        nc.tensor.transpose(cols_ps[:, 0:P], rows[:], ident[:])
-        cols = held.tile([P, NVEC], F32, name="cols")
-        nc.vector.tensor_copy(cols[:], cols_ps[:, 0:NVEC])
-
-        for i in range(NLN):
-            piece = slice(i * LNW, (i + 1) * LNW)
-            nc.gpsimd.tensor_tensor(squared_sum[:, piece], squared[:, 0, piece], squared[:, 1, piece], ALU.add)
-            var_ps = psum.tile([P, TOK], F32, name="var_ps", tag="bank")
-            nc.tensor.matmul(var_ps[:, 0:LNW], averager[:], squared_sum[:, piece], start=True, stop=True)
-            nc.scalar.activation(rstd[:, piece], var_ps[:, 0:LNW], ACT.Abs_reciprocal_sqrt, bias=eps_col[:])
-            rstd_both = rstd[:, piece].unsqueeze(1).to_broadcast([P, CB, LNW])
-            nc.vector.tensor_tensor(centered[:, :, piece], centered[:, :, piece], rstd_both, ALU.mult)
-            for cb in range(CB):
-                nc.vector.tensor_scalar(
-                    nrm[:, cb, piece],
-                    centered[:, cb, piece],
-                    cols[:, GAIN + cb : GAIN + cb + 1],
-                    cols[:, BIAS + cb : BIAS + cb + 1],
-                    ALU.mult,
-                    ALU.add,
-                )
+        def layer_norm_back(n):
+            pieces = range(n * PIECES, (n + 1) * PIECES)
+            turned_back = {}
+            for i in pieces:
+                for k in range(PAIR):
+                    t = i * PAIR + k
+                    nc.vector.tensor_scalar(
+                        x_hat[:, t, :],
+                        x_turned[i][:, k * C : (k + 1) * C],
+                        mean_var[:, t, 0:1],
+                        rstd[:, t : t + 1],
+                        ALU.subtract,
+                        ALU.mult,
+                    )
+                turned_back[i] = psum.tile([P, TOK], F32, name="turned_back", tag="bank")
+                for k in range(PAIR):
+                    t = i * PAIR + k
+                    for cb in range(CB):
+                        tokens = slice(cb * LNW + k * P, cb * LNW + (k + 1) * P)
+                        nc.tensor.transpose(turned_back[i][:, tokens], x_hat[:, t, cb * P : (cb + 1) * P], ident[:])
+            for i in pieces:
+                for cb in range(CB):
+                    nc.vector.tensor_scalar(
+                        nrm[:, cb, i * LNW : (i + 1) * LNW],
+                        turned_back[i][:, cb * LNW : (cb + 1) * LNW],
+                        gain_col[:, cb : cb + 1],
+                        bias_col[:, cb : cb + 1],
+                        ALU.mult,
+                        ALU.add,
+                    )
 
         hidden = held.tile([P, FB, N], BF16, name="hidden")
         mlp = [held.tile([P, N], F32, name=f"mlp{cb}") for cb in range(CB)]
@@ -113,7 +133,7 @@ def tile_stoichiometricmab_kernel(tc, base, x, ln_gain, ln_bias, w1, b1, w2, b2,
                     nc.tensor.matmul(
                         h_ps[:], w1_sb[:, cb, fb * P : (fb + 1) * P], nrm[:, cb, chunk], start=(cb == 0), stop=(cb == CB - 1)
                     )
-                nc.scalar.activation(hidden[:, fb, chunk], h_ps[:], ACT.Gelu, bias=cols[:, B1 + fb : B1 + fb + 1])
+                nc.scalar.activation(hidden[:, fb, chunk], h_ps[:], ACT.Gelu, bias=b1_col[:, fb : fb + 1])
 
         def second_matmul(n, cb):
             chunk = slice(n * TOK, (n + 1) * TOK)
@@ -122,21 +142,24 @@ def tile_stoichiometricmab_kernel(tc, base, x, ln_gain, ln_bias, w1, b1, w2, b2,
                 nc.tensor.matmul(
                     mlp_ps[:], w2_sb[:, fb, cb * P : (cb + 1) * P], hidden[:, fb, chunk], start=(fb == 0), stop=(fb == FB - 1)
                 )
-            b2_col = cols[:, B2 + cb : B2 + cb + 1]
             if cb == 0:
-                nc.vector.tensor_scalar_add(mlp[cb][:, chunk], mlp_ps[:], b2_col)
+                nc.vector.tensor_scalar_add(mlp[cb][:, chunk], mlp_ps[:], b2_col[:, cb : cb + 1])
             else:
-                nc.scalar.activation(mlp[cb][:, chunk], mlp_ps[:], ACT.Identity, bias=b2_col)
+                nc.scalar.activation(mlp[cb][:, chunk], mlp_ps[:], ACT.Identity, bias=b2_col[:, cb : cb + 1])
 
         def place(cb):
             nc.vector.tensor_tensor(window[cb][:].indirect(offsets[:]), mlp[cb][:], x_sb[:, cb, :], ALU.add)
             nc.sync.dma_start(out[cb * P : (cb + 1) * P, :], window[cb][:])
 
-        first_matmul(0)
-        for n in range(1, NCH):
+        layer_norm_front(0)
+        layer_norm_back(0)
+        for n in range(NCH):
+            if n + 1 < NCH:
+                layer_norm_front(n + 1)
             first_matmul(n)
-            second_matmul(n - 1, 0)
-        second_matmul(NCH - 1, 0)
+            if n + 1 < NCH:
+                layer_norm_back(n + 1)
+            second_matmul(n, 0)
         place(0)
         for n in range(NCH):
             second_matmul(n, 1)

@@ -30,6 +30,8 @@ def tile_stoichiometricmab_kernel(tc, base, x, ln_gain, ln_bias, w1, b1, w2, b2,
     ):
         ident = held.tile([P, P], F32, name="ident")
         make_identity(nc, ident[:])
+        ident_bf = held.tile([P, P], BF16, name="ident_bf")
+        make_identity(nc, ident_bf[:])
         minus_half = held.tile([P, PAIR], F32, name="minus_half")
         nc.vector.memset(minus_half[:], -0.5)
 
@@ -47,8 +49,10 @@ def tile_stoichiometricmab_kernel(tc, base, x, ln_gain, ln_bias, w1, b1, w2, b2,
 
         load_x(0)
         load_x(1)
-        gain_col = load_columns(ln_gain, CB, "gain_col")
-        bias_col = load_columns(ln_bias, CB, "bias_col")
+        gain_row = held.tile([P, C], F32, name="gain_row")
+        nc.sync.dma_start(gain_row[:], ln_gain.rearrange("c o -> (c o)").partition_broadcast(P))
+        bias_row = held.tile([P, C], F32, name="bias_row")
+        nc.sync.dma_start(bias_row[:], ln_bias.rearrange("c o -> (c o)").partition_broadcast(P))
         w1_sb = held.tile([P, CB, F], BF16, name="w1_sb")
         nc.sync.dma_start(w1_sb[:], w1.rearrange("(cb p) f -> p cb f", p=P))
         b1_col = load_columns(b1, FB, "b1_col")
@@ -69,7 +73,8 @@ def tile_stoichiometricmab_kernel(tc, base, x, ln_gain, ln_bias, w1, b1, w2, b2,
         mean_var = held.tile([P, NT, 2], F32, name="mean_var")
         var_eps = held.tile([P, NT], F32, name="var_eps")
         rstd = held.tile([P, NT], F32, name="rstd")
-        x_hat = held.tile([P, NT, C], F32, name="x_hat")
+        scaled = held.tile([P, NT, C], F32, name="scaled")
+        nrm_turned = held.tile([P, NT, C], BF16, name="nrm_turned")
         nrm = held.tile([P, CB, N], BF16, name="nrm")
         x_turned = {}
 
@@ -93,34 +98,28 @@ def tile_stoichiometricmab_kernel(tc, base, x, ln_gain, ln_bias, w1, b1, w2, b2,
 
         def layer_norm_back(n):
             pieces = range(n * PIECES, (n + 1) * PIECES)
+            for i in pieces:
+                for k in range(PAIR):
+                    t = i * PAIR + k
+                    nc.vector.scalar_tensor_tensor(
+                        scaled[:, t, :], x_turned[i][:, k * C : (k + 1) * C], mean_var[:, t, 0:1], gain_row[:], ALU.subtract, ALU.mult
+                    )
             turned_back = {}
             for i in pieces:
                 for k in range(PAIR):
                     t = i * PAIR + k
-                    nc.vector.tensor_scalar(
-                        x_hat[:, t, :],
-                        x_turned[i][:, k * C : (k + 1) * C],
-                        mean_var[:, t, 0:1],
-                        rstd[:, t : t + 1],
-                        ALU.subtract,
-                        ALU.mult,
+                    nc.vector.scalar_tensor_tensor(
+                        nrm_turned[:, t, :], scaled[:, t, :], rstd[:, t : t + 1], bias_row[:], ALU.mult, ALU.add
                     )
-                turned_back[i] = psum.tile([P, TOK], F32, name="turned_back", tag="bank")
+                turned_back[i] = psum.tile([P, CB, LNW], BF16, name="turned_back", tag="bank")
                 for k in range(PAIR):
                     t = i * PAIR + k
                     for cb in range(CB):
-                        tokens = slice(cb * LNW + k * P, cb * LNW + (k + 1) * P)
-                        nc.tensor.transpose(turned_back[i][:, tokens], x_hat[:, t, cb * P : (cb + 1) * P], ident[:])
+                        nc.tensor.transpose(
+                            turned_back[i][:, cb, k * P : (k + 1) * P], nrm_turned[:, t, cb * P : (cb + 1) * P], ident_bf[:]
+                        )
             for i in pieces:
-                for cb in range(CB):
-                    nc.vector.tensor_scalar(
-                        nrm[:, cb, i * LNW : (i + 1) * LNW],
-                        turned_back[i][:, cb * LNW : (cb + 1) * LNW],
-                        gain_col[:, cb : cb + 1],
-                        bias_col[:, cb : cb + 1],
-                        ALU.mult,
-                        ALU.add,
-                    )
+                nc.vector.tensor_copy(nrm[:, :, i * LNW : (i + 1) * LNW], turned_back[i][:])
 
         hidden = held.tile([P, FB, N], BF16, name="hidden")
         mlp = [held.tile([P, N], F32, name=f"mlp{cb}") for cb in range(CB)]

@@ -96,21 +96,23 @@ def tile_stoichiometricmab_kernel(tc, base, x, ln_gain, ln_bias, w1, b1, w2, b2,
                 nc.gpsimd.tensor_scalar_add(var_eps[:, pair], mean_var[:, pair, 1], EPS)
                 nc.gpsimd.tensor_tensor(rstd[:, pair], var_eps[:, pair], minus_half[:], ALU.pow)
 
-        def layer_norm_back(n):
-            pieces = range(n * PIECES, (n + 1) * PIECES)
             for i in pieces:
                 for k in range(PAIR):
                     t = i * PAIR + k
                     nc.vector.scalar_tensor_tensor(
                         scaled[:, t, :], x_turned[i][:, k * C : (k + 1) * C], mean_var[:, t, 0:1], gain_row[:], ALU.subtract, ALU.mult
                     )
-            turned_back = {}
             for i in pieces:
                 for k in range(PAIR):
                     t = i * PAIR + k
                     nc.vector.scalar_tensor_tensor(
                         nrm_turned[:, t, :], scaled[:, t, :], rstd[:, t : t + 1], bias_row[:], ALU.mult, ALU.add
                     )
+
+        def layer_norm_back(n):
+            pieces = range(n * PIECES, (n + 1) * PIECES)
+            turned_back = {}
+            for i in pieces:
                 turned_back[i] = psum.tile([P, CB, LNW], BF16, name="turned_back", tag="bank")
                 for k in range(PAIR):
                     t = i * PAIR + k
@@ -134,10 +136,12 @@ def tile_stoichiometricmab_kernel(tc, base, x, ln_gain, ln_bias, w1, b1, w2, b2,
                     )
                 nc.scalar.activation(hidden[:, fb, chunk], h_ps[:], ACT.Gelu, bias=b1_col[:, fb : fb + 1])
 
-        def second_matmul(n, cb):
+        def second_matmul(n, cb, back_of=None):
             chunk = slice(n * TOK, (n + 1) * TOK)
             mlp_ps = psum.tile([P, TOK], F32, name="mlp_ps", tag="bank")
             for fb in range(FB):
+                if fb == FB // 2 and back_of is not None:
+                    layer_norm_back(back_of)
                 nc.tensor.matmul(
                     mlp_ps[:], w2_sb[:, fb, cb * P : (cb + 1) * P], hidden[:, fb, chunk], start=(fb == 0), stop=(fb == FB - 1)
                 )
@@ -152,13 +156,12 @@ def tile_stoichiometricmab_kernel(tc, base, x, ln_gain, ln_bias, w1, b1, w2, b2,
 
         layer_norm_front(0)
         layer_norm_back(0)
+        layer_norm_front(1)
         for n in range(NCH):
-            if n + 1 < NCH:
-                layer_norm_front(n + 1)
             first_matmul(n)
-            if n + 1 < NCH:
-                layer_norm_back(n + 1)
-            second_matmul(n, 0)
+            second_matmul(n, 0, back_of=(n + 1 if n + 1 < NCH else None))
+            if n + 2 < NCH:
+                layer_norm_front(n + 2)
         place(0)
         for n in range(NCH):
             second_matmul(n, 1)

@@ -15,8 +15,9 @@ TOK = 512
 NCH = N // TOK
 NT = N // P
 PAIR = TOK // C
-LNW = PAIR * P
-PIECES = TOK // LNW
+TILES = TOK // P
+STEPS = TILES * CB
+assert FB * CB == 2 * STEPS
 EPS = 1e-5
 
 FLOPS = 2 * N * C * F * 2
@@ -77,51 +78,48 @@ def tile_stoichiometricmab_kernel(tc, base, x, ln_gain, ln_bias, w1, b1, w2, b2,
         nrm_turned = held.tile([P, NT, C], BF16, name="nrm_turned")
         nrm = held.tile([P, CB, N], BF16, name="nrm")
         x_turned = {}
+        turned_back = {}
 
-        def layer_norm_front(n):
-            pieces = range(n * PIECES, (n + 1) * PIECES)
-            for i in pieces:
+        def turn(n, step):
+            t, cb = n * TILES + step // CB, step % CB
+            i, k = t // PAIR, t % PAIR
+            if k == 0 and cb == 0:
                 x_turned[i] = psum.tile([P, TOK], F32, name="x_turned", tag="bank")
-                for k in range(PAIR):
-                    tokens = slice((i * PAIR + k) * P, (i * PAIR + k + 1) * P)
-                    for cb in range(CB):
-                        channels = slice(k * C + cb * P, k * C + (cb + 1) * P)
-                        nc.tensor.transpose(x_turned[i][:, channels], x_sb[:, cb, tokens], ident[:])
-            for i in pieces:
-                for k in range(PAIR):
-                    t = i * PAIR + k
-                    nc.vector.bn_stats(stats[:, t, :], x_turned[i][:, k * C : (k + 1) * C])
-                    nc.vector.bn_aggr(mean_var[:, t, :], stats[:, t, :])
-                pair = slice(i * PAIR, (i + 1) * PAIR)
-                nc.gpsimd.tensor_scalar_add(var_eps[:, pair], mean_var[:, pair, 1], EPS)
-                nc.gpsimd.tensor_tensor(rstd[:, pair], var_eps[:, pair], minus_half[:], ALU.pow)
+            nc.tensor.transpose(x_turned[i][:, k * C + cb * P : k * C + (cb + 1) * P], x_sb[:, cb, t * P : (t + 1) * P], ident[:])
 
-            for i in pieces:
-                for k in range(PAIR):
-                    t = i * PAIR + k
-                    nc.vector.scalar_tensor_tensor(
-                        scaled[:, t, :], x_turned[i][:, k * C : (k + 1) * C], mean_var[:, t, 0:1], gain_row[:], ALU.subtract, ALU.mult
-                    )
-            for i in pieces:
-                for k in range(PAIR):
-                    t = i * PAIR + k
-                    nc.vector.scalar_tensor_tensor(
-                        nrm_turned[:, t, :], scaled[:, t, :], rstd[:, t : t + 1], bias_row[:], ALU.mult, ALU.add
-                    )
+        def normalise(n):
+            tiles = range(n * TILES, (n + 1) * TILES)
+            for t in tiles:
+                nc.vector.bn_stats(stats[:, t, :], x_turned[t // PAIR][:, (t % PAIR) * C : (t % PAIR + 1) * C])
+                nc.vector.bn_aggr(mean_var[:, t, :], stats[:, t, :])
+                if t % PAIR == PAIR - 1:
+                    pair = slice(t + 1 - PAIR, t + 1)
+                    nc.gpsimd.tensor_scalar_add(var_eps[:, pair], mean_var[:, pair, 1], EPS)
+                    nc.gpsimd.tensor_tensor(rstd[:, pair], var_eps[:, pair], minus_half[:], ALU.pow)
+            for t in tiles:
+                nc.vector.scalar_tensor_tensor(
+                    scaled[:, t, :],
+                    x_turned[t // PAIR][:, (t % PAIR) * C : (t % PAIR + 1) * C],
+                    mean_var[:, t, 0:1],
+                    gain_row[:],
+                    ALU.subtract,
+                    ALU.mult,
+                )
+            for t in tiles:
+                nc.vector.scalar_tensor_tensor(
+                    nrm_turned[:, t, :], scaled[:, t, :], rstd[:, t : t + 1], bias_row[:], ALU.mult, ALU.add
+                )
 
-        def layer_norm_back(n):
-            pieces = range(n * PIECES, (n + 1) * PIECES)
-            turned_back = {}
-            for i in pieces:
-                turned_back[i] = psum.tile([P, CB, LNW], BF16, name="turned_back", tag="bank")
-                for k in range(PAIR):
-                    t = i * PAIR + k
-                    for cb in range(CB):
-                        nc.tensor.transpose(
-                            turned_back[i][:, cb, k * P : (k + 1) * P], nrm_turned[:, t, cb * P : (cb + 1) * P], ident_bf[:]
-                        )
-            for i in pieces:
-                nc.vector.tensor_copy(nrm[:, :, i * LNW : (i + 1) * LNW], turned_back[i][:])
+        def turn_back(n, step):
+            k, cb = step // CB, step % CB
+            if step == 0:
+                turned_back[n] = psum.tile([P, CB, TOK], BF16, name="turned_back", tag="bank")
+            nc.tensor.transpose(
+                turned_back[n][:, cb, k * P : (k + 1) * P], nrm_turned[:, n * TILES + k, cb * P : (cb + 1) * P], ident_bf[:]
+            )
+
+        def copy_back(n):
+            nc.scalar.copy(nrm[:, :, n * TOK : (n + 1) * TOK], turned_back[n][:])
 
         hidden = held.tile([P, FB, N], BF16, name="hidden")
         mlp = [held.tile([P, N], F32, name=f"mlp{cb}") for cb in range(CB)]
@@ -134,14 +132,21 @@ def tile_stoichiometricmab_kernel(tc, base, x, ln_gain, ln_bias, w1, b1, w2, b2,
                     nc.tensor.matmul(
                         h_ps[:], w1_sb[:, cb, fb * P : (fb + 1) * P], nrm[:, cb, chunk], start=(cb == 0), stop=(cb == CB - 1)
                     )
+                    step = fb * CB + cb
+                    if step < STEPS and n + 2 < NCH:
+                        turn(n + 2, step)
+                    if step >= STEPS and n + 1 < NCH:
+                        turn_back(n + 1, step - STEPS)
                 nc.scalar.activation(hidden[:, fb, chunk], h_ps[:], ACT.Gelu, bias=b1_col[:, fb : fb + 1])
+                if fb == FB // 2 - 1 and n + 2 < NCH:
+                    normalise(n + 2)
+            if n + 1 < NCH:
+                copy_back(n + 1)
 
-        def second_matmul(n, cb, back_of=None):
+        def second_matmul(n, cb):
             chunk = slice(n * TOK, (n + 1) * TOK)
             mlp_ps = psum.tile([P, TOK], F32, name="mlp_ps", tag="bank")
             for fb in range(FB):
-                if fb == FB // 2 and back_of is not None:
-                    layer_norm_back(back_of)
                 nc.tensor.matmul(
                     mlp_ps[:], w2_sb[:, fb, cb * P : (cb + 1) * P], hidden[:, fb, chunk], start=(fb == 0), stop=(fb == FB - 1)
                 )
@@ -154,14 +159,16 @@ def tile_stoichiometricmab_kernel(tc, base, x, ln_gain, ln_bias, w1, b1, w2, b2,
             nc.vector.tensor_tensor(window[cb][:].indirect(offsets[:]), mlp[cb][:], x_sb[:, cb, :], ALU.add)
             nc.sync.dma_start(out[cb * P : (cb + 1) * P, :], window[cb][:])
 
-        layer_norm_front(0)
-        layer_norm_back(0)
-        layer_norm_front(1)
+        for n in range(2):
+            for step in range(STEPS):
+                turn(n, step)
+            normalise(n)
+        for step in range(STEPS):
+            turn_back(0, step)
+        copy_back(0)
         for n in range(NCH):
             first_matmul(n)
-            second_matmul(n, 0, back_of=(n + 1 if n + 1 < NCH else None))
-            if n + 2 < NCH:
-                layer_norm_front(n + 2)
+            second_matmul(n, 0)
         place(0)
         for n in range(NCH):
             second_matmul(n, 1)

@@ -31,8 +31,6 @@ def tile_stoichiometricmab_kernel(tc, base, x, ln_gain, ln_bias, w1, b1, w2, b2,
     ):
         ident = held.tile([P, P], F32, name="ident")
         make_identity(nc, ident[:])
-        ident_bf = held.tile([P, P], BF16, name="ident_bf")
-        make_identity(nc, ident_bf[:])
         minus_half = held.tile([P, PAIR], F32, name="minus_half")
         nc.vector.memset(minus_half[:], -0.5)
 
@@ -52,8 +50,7 @@ def tile_stoichiometricmab_kernel(tc, base, x, ln_gain, ln_bias, w1, b1, w2, b2,
         load_x(1)
         gain_row = held.tile([P, C], F32, name="gain_row")
         nc.sync.dma_start(gain_row[:], ln_gain.rearrange("c o -> (c o)").partition_broadcast(P))
-        bias_row = held.tile([P, C], F32, name="bias_row")
-        nc.sync.dma_start(bias_row[:], ln_bias.rearrange("c o -> (c o)").partition_broadcast(P))
+        bias_col = load_columns(ln_bias, CB, "bias_col")
         w1_sb = held.tile([P, CB, F], BF16, name="w1_sb")
         nc.sync.dma_start(w1_sb[:], w1.rearrange("(cb p) f -> p cb f", p=P))
         b1_col = load_columns(b1, FB, "b1_col")
@@ -75,7 +72,7 @@ def tile_stoichiometricmab_kernel(tc, base, x, ln_gain, ln_bias, w1, b1, w2, b2,
         var_eps = held.tile([P, NT], F32, name="var_eps")
         rstd = held.tile([P, NT], F32, name="rstd")
         scaled = held.tile([P, NT, C], F32, name="scaled")
-        nrm_turned = held.tile([P, NT, C], BF16, name="nrm_turned")
+        x_hat = held.tile([P, NT, C], F32, name="x_hat")
         nrm = held.tile([P, CB, N], BF16, name="nrm")
         x_turned = {}
         turned_back = {}
@@ -106,20 +103,19 @@ def tile_stoichiometricmab_kernel(tc, base, x, ln_gain, ln_bias, w1, b1, w2, b2,
                     ALU.mult,
                 )
             for t in tiles:
-                nc.vector.scalar_tensor_tensor(
-                    nrm_turned[:, t, :], scaled[:, t, :], rstd[:, t : t + 1], bias_row[:], ALU.mult, ALU.add
-                )
+                nc.vector.tensor_scalar_mul(x_hat[:, t, :], scaled[:, t, :], rstd[:, t : t + 1])
 
         def turn_back(n, step):
             k, cb = step // CB, step % CB
-            if step == 0:
-                turned_back[n] = psum.tile([P, CB, TOK], BF16, name="turned_back", tag="bank")
-            nc.tensor.transpose(
-                turned_back[n][:, cb, k * P : (k + 1) * P], nrm_turned[:, n * TILES + k, cb * P : (cb + 1) * P], ident_bf[:]
-            )
+            if k == 0:
+                turned_back[n, cb] = psum.tile([P, TOK], F32, name="turned_back", tag="bank")
+            nc.tensor.transpose(turned_back[n, cb][:, k * P : (k + 1) * P], x_hat[:, n * TILES + k, cb * P : (cb + 1) * P], ident[:])
 
-        def copy_back(n):
-            nc.scalar.copy(nrm[:, :, n * TOK : (n + 1) * TOK], turned_back[n][:])
+        def bias_and_round(n):
+            for cb in range(CB):
+                nc.scalar.activation(
+                    nrm[:, cb, n * TOK : (n + 1) * TOK], turned_back[n, cb][:], ACT.Identity, bias=bias_col[:, cb : cb + 1]
+                )
 
         hidden = held.tile([P, FB, N], BF16, name="hidden")
         mlp = [held.tile([P, N], F32, name=f"mlp{cb}") for cb in range(CB)]
@@ -141,7 +137,7 @@ def tile_stoichiometricmab_kernel(tc, base, x, ln_gain, ln_bias, w1, b1, w2, b2,
                 if fb == FB // 2 - 1 and n + 2 < NCH:
                     normalise(n + 2)
             if n + 1 < NCH:
-                copy_back(n + 1)
+                bias_and_round(n + 1)
 
         def second_matmul(n, cb):
             chunk = slice(n * TOK, (n + 1) * TOK)
@@ -165,7 +161,7 @@ def tile_stoichiometricmab_kernel(tc, base, x, ln_gain, ln_bias, w1, b1, w2, b2,
             normalise(n)
         for step in range(STEPS):
             turn_back(0, step)
-        copy_back(0)
+        bias_and_round(0)
         for n in range(NCH):
             first_matmul(n)
             second_matmul(n, 0)

@@ -36,26 +36,27 @@ def tile_stoichiometricmab_kernel(tc, base, x, ln_gain, ln_bias, w1, b1, w2, b2,
 
         x_sb = held.tile([P, CB, N], F32, name="x_sb")
 
-        def load_x(n):
-            chunk = slice(n * TOK, (n + 1) * TOK)
-            nc.sync.dma_start(x_sb[:, 0, chunk], x[0:P, chunk])
-            nc.scalar.dma_start(x_sb[:, 1, chunk], x[P : 2 * P, chunk])
+        def load_x(first_token, tokens):
+            part = slice(first_token, first_token + tokens)
+            nc.sync.dma_start(x_sb[:, 0, part], x[0:P, part])
+            nc.scalar.dma_start(x_sb[:, 1, part], x[P : 2 * P, part])
 
         def load_columns(vector, blocks, name):
             columns = held.tile([P, blocks], F32, name=name)
             nc.sync.dma_start(columns[:], vector.rearrange("(r p) o -> p (r o)", p=P))
             return columns
 
-        load_x(0)
-        load_x(1)
+        load_x(0, TOK // 2)
+        load_x(TOK // 2, TOK // 2)
+        load_x(TOK, TOK)
         gain_row = held.tile([P, C], F32, name="gain_row")
         nc.sync.dma_start(gain_row[:], ln_gain.rearrange("c o -> (c o)").partition_broadcast(P))
         bias_col = load_columns(ln_bias, CB, "bias_col")
         w1_sb = held.tile([P, CB, F], BF16, name="w1_sb")
         nc.sync.dma_start(w1_sb[:], w1.rearrange("(cb p) f -> p cb f", p=P))
         b1_col = load_columns(b1, FB, "b1_col")
-        load_x(2)
-        load_x(3)
+        load_x(2 * TOK, TOK)
+        load_x(3 * TOK, TOK)
         w2_sb = held.tile([P, FB, C], BF16, name="w2_sb")
         nc.sync.dma_start(w2_sb[:], w2.rearrange("(fb p) c -> p fb c", p=P))
         b2_col = load_columns(b2, CB, "b2_col")

@@ -107,15 +107,16 @@ def tile_stoichiometricmab_kernel(tc, base, x, ln_gain, ln_bias, w1, b1, w2, b2,
                 nc.vector.tensor_scalar_mul(x_hat[:, t, :], scaled[:, t, :], rstd[:, t : t + 1])
 
         def turn_back(n, step):
-            k, cb = step // CB, step % CB
-            if k == 0:
-                turned_back[n, cb] = psum.tile([P, TOK], F32, name="turned_back", tag="bank")
-            nc.tensor.transpose(turned_back[n, cb][:, k * P : (k + 1) * P], x_hat[:, n * TILES + k, cb * P : (cb + 1) * P], ident[:])
+            t, cb = n * TILES + step // CB, step % CB
+            i, k = t // PAIR, t % PAIR
+            if k == 0 and cb == 0:
+                turned_back[i] = psum.tile([P, CB, PAIR * P], F32, name="turned_back", tag="bank")
+            nc.tensor.transpose(turned_back[i][:, cb, k * P : (k + 1) * P], x_hat[:, t, cb * P : (cb + 1) * P], ident[:])
 
-        def bias_and_round(n):
+        def bias_and_round(i):
             for cb in range(CB):
                 nc.scalar.activation(
-                    nrm[:, cb, n * TOK : (n + 1) * TOK], turned_back[n, cb][:], ACT.Identity, bias=bias_col[:, cb : cb + 1]
+                    nrm[:, cb, i * PAIR * P : (i + 1) * PAIR * P], turned_back[i][:, cb, :], ACT.Identity, bias=bias_col[:, cb : cb + 1]
                 )
 
         hidden = held.tile([P, FB, N], BF16, name="hidden")
@@ -137,8 +138,9 @@ def tile_stoichiometricmab_kernel(tc, base, x, ln_gain, ln_bias, w1, b1, w2, b2,
                 nc.scalar.activation(hidden[:, fb, chunk], h_ps[:], ACT.Gelu, bias=b1_col[:, fb : fb + 1])
                 if fb == FB // 2 - 1 and n + 2 < NCH:
                     normalise(n + 2)
-            if n + 1 < NCH:
-                bias_and_round(n + 1)
+                back = (fb + 1) * CB - STEPS
+                if back > 0 and back % (PAIR * CB) == 0 and n + 1 < NCH:
+                    bias_and_round(((n + 1) * STEPS + back) // (PAIR * CB) - 1)
 
         def second_matmul(n, cb):
             chunk = slice(n * TOK, (n + 1) * TOK)
@@ -162,7 +164,8 @@ def tile_stoichiometricmab_kernel(tc, base, x, ln_gain, ln_bias, w1, b1, w2, b2,
             normalise(n)
         for step in range(STEPS):
             turn_back(0, step)
-        bias_and_round(0)
+            if (step + 1) % (PAIR * CB) == 0:
+                bias_and_round(step // (PAIR * CB))
         for n in range(NCH):
             first_matmul(n)
             second_matmul(n, 0)

@@ -16,6 +16,7 @@ NCH = N // TOK
 NT = N // P
 PAIR = TOK // C
 TILES = TOK // P
+CHUNK_PAIRS = TILES // PAIR
 STEPS = TILES * CB
 assert FB * CB == 2 * STEPS
 EPS = 1e-5
@@ -33,13 +34,19 @@ def tile_stoichiometricmab_kernel(tc, base, x, ln_gain, ln_bias, w1, b1, w2, b2,
         make_identity(nc, ident[:])
         minus_half = held.tile([P, PAIR], F32, name="minus_half")
         nc.vector.memset(minus_half[:], -0.5)
+        eps_col = held.tile([P, 1], F32, name="eps_col")
+        nc.vector.memset(eps_col[:], EPS)
+        one = held.tile([P, 1], F32, name="one")
+        nc.vector.memset(one[:], 1.0)
+        table_warm = held.tile([P, 2], F32, name="table_warm")
+        nc.scalar.activation(table_warm[:, 0:1], one[:], ACT.Abs_reciprocal_sqrt)
 
         x_sb = held.tile([P, CB, N], F32, name="x_sb")
+        x_blocks = x.rearrange("(cb p) n -> p cb n", p=P)
 
         def load_x(first_token, tokens):
             part = slice(first_token, first_token + tokens)
-            nc.sync.dma_start(x_sb[:, 0, part], x[0:P, part])
-            nc.scalar.dma_start(x_sb[:, 1, part], x[P : 2 * P, part])
+            nc.sync.dma_start(x_sb[:, :, part], x_blocks[:, :, part])
 
         def load_columns(vector, blocks, name):
             columns = held.tile([P, blocks], F32, name=name)
@@ -49,8 +56,7 @@ def tile_stoichiometricmab_kernel(tc, base, x, ln_gain, ln_bias, w1, b1, w2, b2,
         load_x(0, TOK // 2)
         load_x(TOK // 2, TOK // 2)
         load_x(TOK, TOK)
-        gain_row = held.tile([P, C], F32, name="gain_row")
-        nc.sync.dma_start(gain_row[:], ln_gain.rearrange("c o -> (c o)").partition_broadcast(P))
+        gain_col = load_columns(ln_gain, CB, "gain_col")
         bias_col = load_columns(ln_bias, CB, "bias_col")
         w1_sb = held.tile([P, CB, F], BF16, name="w1_sb")
         nc.sync.dma_start(w1_sb[:], w1.rearrange("(cb p) f -> p cb f", p=P))
@@ -72,7 +78,6 @@ def tile_stoichiometricmab_kernel(tc, base, x, ln_gain, ln_bias, w1, b1, w2, b2,
         mean_var = held.tile([P, NT, 2], F32, name="mean_var")
         var_eps = held.tile([P, NT], F32, name="var_eps")
         rstd = held.tile([P, NT], F32, name="rstd")
-        scaled = held.tile([P, NT, C], F32, name="scaled")
         x_hat = held.tile([P, NT, C], F32, name="x_hat")
         nrm = held.tile([P, CB, N], BF16, name="nrm")
         x_turned = {}
@@ -87,24 +92,32 @@ def tile_stoichiometricmab_kernel(tc, base, x, ln_gain, ln_bias, w1, b1, w2, b2,
 
         def normalise(n):
             tiles = range(n * TILES, (n + 1) * TILES)
-            for t in tiles:
-                nc.vector.bn_stats(stats[:, t, :], x_turned[t // PAIR][:, (t % PAIR) * C : (t % PAIR + 1) * C])
+            def aggregate(t):
                 nc.vector.bn_aggr(mean_var[:, t, :], stats[:, t, :])
                 if t % PAIR == PAIR - 1:
                     pair = slice(t + 1 - PAIR, t + 1)
-                    nc.gpsimd.tensor_scalar_add(var_eps[:, pair], mean_var[:, pair, 1], EPS)
-                    nc.gpsimd.tensor_tensor(rstd[:, pair], var_eps[:, pair], minus_half[:], ALU.pow)
+                    if n == 0:
+                        nc.scalar.activation(rstd[:, pair], mean_var[:, pair, 1], ACT.Abs_reciprocal_sqrt, bias=eps_col[:])
+                        if t == tiles[-1]:
+                            nc.scalar.activation(table_warm[:, 1:2], rstd[:, t : t + 1], ACT.Gelu)
+                    else:
+                        nc.gpsimd.tensor_scalar_add(var_eps[:, pair], mean_var[:, pair, 1], EPS)
+                        nc.gpsimd.tensor_tensor(rstd[:, pair], var_eps[:, pair], minus_half[:], ALU.pow)
+
             for t in tiles:
-                nc.vector.scalar_tensor_tensor(
-                    scaled[:, t, :],
+                nc.vector.bn_stats(stats[:, t, :], x_turned[t // PAIR][:, (t % PAIR) * C : (t % PAIR + 1) * C])
+                if t > tiles[0]:
+                    aggregate(t - 1)
+            aggregate(tiles[-1])
+            for t in tiles:
+                nc.vector.tensor_scalar(
+                    x_hat[:, t, :],
                     x_turned[t // PAIR][:, (t % PAIR) * C : (t % PAIR + 1) * C],
                     mean_var[:, t, 0:1],
-                    gain_row[:],
+                    rstd[:, t : t + 1],
                     ALU.subtract,
                     ALU.mult,
                 )
-            for t in tiles:
-                nc.vector.tensor_scalar_mul(x_hat[:, t, :], scaled[:, t, :], rstd[:, t : t + 1])
 
         def turn_back(n, step):
             t, cb = n * TILES + step // CB, step % CB
@@ -113,42 +126,55 @@ def tile_stoichiometricmab_kernel(tc, base, x, ln_gain, ln_bias, w1, b1, w2, b2,
                 turned_back[i] = psum.tile([P, CB, PAIR * P], F32, name="turned_back", tag="bank")
             nc.tensor.transpose(turned_back[i][:, cb, k * P : (k + 1) * P], x_hat[:, t, cb * P : (cb + 1) * P], ident[:])
 
-        def bias_and_round(i):
+        def gain_bias_round(i):
             for cb in range(CB):
-                nc.scalar.activation(
-                    nrm[:, cb, i * PAIR * P : (i + 1) * PAIR * P], turned_back[i][:, cb, :], ACT.Identity, bias=bias_col[:, cb : cb + 1]
-                )
+                part = slice(i * PAIR * P, (i + 1) * PAIR * P)
+                if i < CHUNK_PAIRS:
+                    nc.vector.tensor_scalar(
+                        nrm[:, cb, part], turned_back[i][:, cb, :], gain_col[:, cb : cb + 1], bias_col[:, cb : cb + 1], ALU.mult, ALU.add
+                    )
+                else:
+                    nc.scalar.activation(
+                        nrm[:, cb, part], turned_back[i][:, cb, :], ACT.Identity, bias=bias_col[:, cb : cb + 1], scale=gain_col[:, cb : cb + 1]
+                    )
+
+        def turning(n):
+            return [(turn, n, step) for step in range(STEPS)]
+
+        def turning_back(n):
+            return [(turn_back, n, step) for step in range(STEPS)]
+
+        def ride(riders, count):
+            for work, n, step in riders[:count]:
+                work(n, step)
+                if work == turn_back and (step + 1) % (PAIR * CB) == 0:
+                    gain_bias_round(n * CHUNK_PAIRS + step // (PAIR * CB))
+            riders[:count] = []
 
         hidden = held.tile([P, FB, N], BF16, name="hidden")
         mlp = [held.tile([P, N], F32, name=f"mlp{cb}") for cb in range(CB)]
 
-        def first_matmul(n):
+        def first_matmul(n, riders):
             chunk = slice(n * TOK, (n + 1) * TOK)
+            riders = list(riders)
             for fb in range(FB):
                 h_ps = psum.tile([P, TOK], F32, name="h_ps", tag="bank")
                 for cb in range(CB):
                     nc.tensor.matmul(
                         h_ps[:], w1_sb[:, cb, fb * P : (fb + 1) * P], nrm[:, cb, chunk], start=(cb == 0), stop=(cb == CB - 1)
                     )
-                    step = fb * CB + cb
-                    if step < STEPS and n + 2 < NCH:
-                        turn(n + 2, step)
-                    if step >= STEPS and n + 1 < NCH:
-                        turn_back(n + 1, step - STEPS)
+                    ride(riders, 1)
                 nc.scalar.activation(hidden[:, fb, chunk], h_ps[:], ACT.Gelu, bias=b1_col[:, fb : fb + 1])
-                if fb == FB // 2 - 1 and n + 2 < NCH:
-                    normalise(n + 2)
-                back = (fb + 1) * CB - STEPS
-                if back > 0 and back % (PAIR * CB) == 0 and n + 1 < NCH:
-                    bias_and_round(((n + 1) * STEPS + back) // (PAIR * CB) - 1)
 
-        def second_matmul(n, cb):
+        def second_matmul(n, cb, riders):
             chunk = slice(n * TOK, (n + 1) * TOK)
+            riders = list(riders)
             mlp_ps = psum.tile([P, TOK], F32, name="mlp_ps", tag="bank")
             for fb in range(FB):
                 nc.tensor.matmul(
                     mlp_ps[:], w2_sb[:, fb, cb * P : (cb + 1) * P], hidden[:, fb, chunk], start=(fb == 0), stop=(fb == FB - 1)
                 )
+                ride(riders, 2)
             if cb == 0:
                 nc.vector.tensor_scalar_add(mlp[cb][:, chunk], mlp_ps[:], b2_col[:, cb : cb + 1])
             else:
@@ -158,18 +184,22 @@ def tile_stoichiometricmab_kernel(tc, base, x, ln_gain, ln_bias, w1, b1, w2, b2,
             nc.vector.tensor_tensor(window[cb][:].indirect(offsets[:]), mlp[cb][:], x_sb[:, cb, :], ALU.add)
             nc.sync.dma_start(out[cb * P : (cb + 1) * P, :], window[cb][:])
 
-        for n in range(2):
-            for step in range(STEPS):
-                turn(n, step)
-            normalise(n)
-        for step in range(STEPS):
-            turn_back(0, step)
-            if (step + 1) % (PAIR * CB) == 0:
-                bias_and_round(step // (PAIR * CB))
-        for n in range(NCH):
-            first_matmul(n)
-            second_matmul(n, 0)
+        ride(turning(0), STEPS)
+        normalise(0)
+        ride(turning(1), STEPS)
+        ride(turning_back(0), STEPS)
+        normalise(1)
+        first_matmul(0, turning(2))
+        second_matmul(0, 0, turning_back(1))
+        normalise(2)
+        first_matmul(1, turning(3) + turning_back(2))
+        second_matmul(1, 0, [])
+        normalise(3)
+        first_matmul(2, turning_back(3))
+        second_matmul(2, 0, [])
+        first_matmul(3, [])
+        second_matmul(3, 0, [])
         place(0)
         for n in range(NCH):
-            second_matmul(n, 1)
+            second_matmul(n, 1, [])
         place(1)

@@ -101,7 +101,7 @@ def tile_stoichiometricmab_kernel(tc, base, x, ln_gain, ln_bias, w1, b1, w2, b2,
                         if t == tiles[-1]:
                             nc.scalar.activation(table_warm[:, 1:2], rstd[:, t : t + 1], ACT.Gelu)
                     else:
-                        nc.gpsimd.tensor_scalar_add(var_eps[:, pair], mean_var[:, pair, 1], EPS)
+                        nc.vector.tensor_scalar_add(var_eps[:, pair], mean_var[:, pair, 1], EPS)
                         nc.gpsimd.tensor_tensor(rstd[:, pair], var_eps[:, pair], minus_half[:], ALU.pow)
 
             for t in tiles:
@@ -129,7 +129,7 @@ def tile_stoichiometricmab_kernel(tc, base, x, ln_gain, ln_bias, w1, b1, w2, b2,
         def gain_bias_round(i):
             for cb in range(CB):
                 part = slice(i * PAIR * P, (i + 1) * PAIR * P)
-                if i < CHUNK_PAIRS:
+                if i == 0:
                     nc.vector.tensor_scalar(
                         nrm[:, cb, part], turned_back[i][:, cb, :], gain_col[:, cb : cb + 1], bias_col[:, cb : cb + 1], ALU.mult, ALU.add
                     )
@@ -166,15 +166,13 @@ def tile_stoichiometricmab_kernel(tc, base, x, ln_gain, ln_bias, w1, b1, w2, b2,
                     ride(riders, 1)
                 nc.scalar.activation(hidden[:, fb, chunk], h_ps[:], ACT.Gelu, bias=b1_col[:, fb : fb + 1])
 
-        def second_matmul(n, cb, riders):
+        def second_matmul(n, cb):
             chunk = slice(n * TOK, (n + 1) * TOK)
-            riders = list(riders)
             mlp_ps = psum.tile([P, TOK], F32, name="mlp_ps", tag="bank")
             for fb in range(FB):
                 nc.tensor.matmul(
                     mlp_ps[:], w2_sb[:, fb, cb * P : (cb + 1) * P], hidden[:, fb, chunk], start=(fb == 0), stop=(fb == FB - 1)
                 )
-                ride(riders, 2)
             if cb == 0:
                 nc.vector.tensor_scalar_add(mlp[cb][:, chunk], mlp_ps[:], b2_col[:, cb : cb + 1])
             else:
@@ -189,17 +187,17 @@ def tile_stoichiometricmab_kernel(tc, base, x, ln_gain, ln_bias, w1, b1, w2, b2,
         ride(turning(1), STEPS)
         ride(turning_back(0), STEPS)
         normalise(1)
-        first_matmul(0, turning(2))
-        second_matmul(0, 0, turning_back(1))
+        first_matmul(0, turning(2) + turning_back(1))
+        second_matmul(0, 0)
         normalise(2)
         first_matmul(1, turning(3) + turning_back(2))
-        second_matmul(1, 0, [])
+        second_matmul(1, 0)
         normalise(3)
         first_matmul(2, turning_back(3))
-        second_matmul(2, 0, [])
+        second_matmul(2, 0)
         first_matmul(3, [])
-        second_matmul(3, 0, [])
+        second_matmul(3, 0)
         place(0)
         for n in range(NCH):
-            second_matmul(n, 1, [])
+            second_matmul(n, 1)
         place(1)

@@ -155,16 +155,33 @@ def tile_stoichiometricmab_kernel(tc, base, x, ln_gain, ln_bias, w1, b1, w2, b2,
         mlp = [held.tile([P, N], F32, name=f"mlp{cb}") for cb in range(CB)]
 
         def first_matmul(n, riders):
-            chunk = slice(n * TOK, (n + 1) * TOK)
-            riders = list(riders)
-            for fb in range(FB):
-                h_ps = psum.tile([P, TOK], F32, name="h_ps", tag="bank")
+            h_ps = {}
+
+            def multiply(fb, first_token, tokens):
+                part = slice(n * TOK + first_token, n * TOK + first_token + tokens)
                 for cb in range(CB):
                     nc.tensor.matmul(
-                        h_ps[:], w1_sb[:, cb, fb * P : (fb + 1) * P], nrm[:, cb, chunk], start=(cb == 0), stop=(cb == CB - 1)
+                        h_ps[fb][:, first_token : first_token + tokens],
+                        w1_sb[:, cb, fb * P : (fb + 1) * P],
+                        nrm[:, cb, part],
+                        start=(cb == 0),
+                        stop=(cb == CB - 1),
                     )
-                    ride(riders, 1)
-                nc.scalar.activation(hidden[:, fb, chunk], h_ps[:], ACT.Gelu, bias=b1_col[:, fb : fb + 1])
+                    if tokens == TOK:
+                        matmuls_left = (FB - fb) * CB - cb
+                        ride(riders, 2 if len(riders) > matmuls_left else 1)
+
+            split = 2 if n == 0 else 0
+            for fb in range(split):
+                h_ps[fb] = psum.tile([P, TOK], F32, name="h_ps", tag="bank")
+                multiply(fb, 0, PAIR * P)
+            for fb in range(FB):
+                if fb < split:
+                    multiply(fb, PAIR * P, PAIR * P)
+                else:
+                    h_ps[fb] = psum.tile([P, TOK], F32, name="h_ps", tag="bank")
+                    multiply(fb, 0, TOK)
+                nc.scalar.activation(hidden[:, fb, n * TOK : (n + 1) * TOK], h_ps[fb][:], ACT.Gelu, bias=b1_col[:, fb : fb + 1])
 
         def second_matmul(n, cb):
             chunk = slice(n * TOK, (n + 1) * TOK)

@@ -154,67 +154,70 @@ def tile_stoichiometricmab_kernel(tc, base, x, ln_gain, ln_bias, w1, b1, w2, b2,
         hidden = held.tile([P, FB, N], BF16, name="hidden")
         mlp = [held.tile([P, N], F32, name=f"mlp{cb}") for cb in range(CB)]
 
-        def first_matmul(n, riders):
+        def first_matmul(tokens, riders, split=0):
             h_ps = {}
+            width = tokens.stop - tokens.start
 
-            def multiply(fb, first_token, tokens):
-                part = slice(n * TOK + first_token, n * TOK + first_token + tokens)
+            def multiply(fb, part):
                 for cb in range(CB):
                     nc.tensor.matmul(
-                        h_ps[fb][:, first_token : first_token + tokens],
+                        h_ps[fb][:, part.start - tokens.start : part.stop - tokens.start],
                         w1_sb[:, cb, fb * P : (fb + 1) * P],
                         nrm[:, cb, part],
                         start=(cb == 0),
                         stop=(cb == CB - 1),
                     )
-                    if tokens == TOK:
+                    if part == tokens:
                         matmuls_left = (FB - fb) * CB - cb
-                        ride(riders, 2 if len(riders) > matmuls_left else 1)
+                        ride(riders, 2 if len(riders) >= 2 * matmuls_left else 1)
 
-            split = 2 if n == 0 else 0
+            middle = tokens.start + PAIR * P
             for fb in range(split):
-                h_ps[fb] = psum.tile([P, TOK], F32, name="h_ps", tag="bank")
-                multiply(fb, 0, PAIR * P)
+                h_ps[fb] = psum.tile([P, width], F32, name="h_ps", tag="bank")
+                multiply(fb, slice(tokens.start, middle))
             for fb in range(FB):
                 if fb < split:
-                    multiply(fb, PAIR * P, PAIR * P)
+                    multiply(fb, slice(middle, tokens.stop))
                 else:
-                    h_ps[fb] = psum.tile([P, TOK], F32, name="h_ps", tag="bank")
-                    multiply(fb, 0, TOK)
-                nc.scalar.activation(hidden[:, fb, n * TOK : (n + 1) * TOK], h_ps[fb][:], ACT.Gelu, bias=b1_col[:, fb : fb + 1])
+                    h_ps[fb] = psum.tile([P, width], F32, name="h_ps", tag="bank")
+                    multiply(fb, tokens)
+                nc.scalar.activation(hidden[:, fb, tokens], h_ps[fb][:], ACT.Gelu, bias=b1_col[:, fb : fb + 1])
 
-        def second_matmul(n, cb):
-            chunk = slice(n * TOK, (n + 1) * TOK)
-            mlp_ps = psum.tile([P, TOK], F32, name="mlp_ps", tag="bank")
+        def second_matmul(tokens, cb):
+            mlp_ps = psum.tile([P, tokens.stop - tokens.start], F32, name="mlp_ps", tag="bank")
             for fb in range(FB):
                 nc.tensor.matmul(
-                    mlp_ps[:], w2_sb[:, fb, cb * P : (cb + 1) * P], hidden[:, fb, chunk], start=(fb == 0), stop=(fb == FB - 1)
+                    mlp_ps[:], w2_sb[:, fb, cb * P : (cb + 1) * P], hidden[:, fb, tokens], start=(fb == 0), stop=(fb == FB - 1)
                 )
             if cb == 0:
-                nc.vector.tensor_scalar_add(mlp[cb][:, chunk], mlp_ps[:], b2_col[:, cb : cb + 1])
+                nc.vector.tensor_scalar_add(mlp[cb][:, tokens], mlp_ps[:], b2_col[:, cb : cb + 1])
             else:
-                nc.scalar.activation(mlp[cb][:, chunk], mlp_ps[:], ACT.Identity, bias=b2_col[:, cb : cb + 1])
+                nc.scalar.activation(mlp[cb][:, tokens], mlp_ps[:], ACT.Identity, bias=b2_col[:, cb : cb + 1])
 
         def place(cb):
             nc.vector.tensor_tensor(window[cb][:].indirect(offsets[:]), mlp[cb][:], x_sb[:, cb, :], ALU.add)
             nc.sync.dma_start(out[cb * P : (cb + 1) * P, :], window[cb][:])
 
+        chunk = [slice(n * TOK, (n + 1) * TOK) for n in range(NCH)]
+        last_pairs = [slice(N - 2 * PAIR * P, N - PAIR * P), slice(N - PAIR * P, N)]
         ride(turning(0), STEPS)
         normalise(0)
         ride(turning(1), STEPS)
         ride(turning_back(0), STEPS)
         normalise(1)
-        first_matmul(0, turning(2) + turning_back(1))
-        second_matmul(0, 0)
+        first_matmul(chunk[0], turning(2) + turning_back(1), split=2)
+        second_matmul(chunk[0], 0)
         normalise(2)
-        first_matmul(1, turning(3) + turning_back(2))
-        second_matmul(1, 0)
+        first_matmul(chunk[1], turning(3) + turning_back(2))
+        second_matmul(chunk[1], 0)
         normalise(3)
-        first_matmul(2, turning_back(3))
-        second_matmul(2, 0)
-        first_matmul(3, [])
-        second_matmul(3, 0)
+        first_matmul(chunk[2], turning_back(3))
+        second_matmul(chunk[2], 0)
+        for pair in last_pairs:
+            first_matmul(pair, [])
+        for pair in last_pairs:
+            second_matmul(pair, 0)
         place(0)
         for n in range(NCH):
-            second_matmul(n, 1)
+            second_matmul(chunk[n], 1)
         place(1)

@@ -129,7 +129,7 @@ def tile_stoichiometricmab_kernel(tc, base, x, ln_gain, ln_bias, w1, b1, w2, b2,
         def gain_bias_round(i):
             for cb in range(CB):
                 part = slice(i * PAIR * P, (i + 1) * PAIR * P)
-                if i == 0:
+                if i == 0 or i >= 2 * CHUNK_PAIRS:
                     nc.vector.tensor_scalar(
                         nrm[:, cb, part], turned_back[i][:, cb, :], gain_col[:, cb : cb + 1], bias_col[:, cb : cb + 1], ALU.mult, ALU.add
                     )
@@ -145,7 +145,7 @@ def tile_stoichiometricmab_kernel(tc, base, x, ln_gain, ln_bias, w1, b1, w2, b2,
             return [(turn_back, n, step) for step in range(STEPS)]
 
         def ride(riders, count):
-            for work, n, step in riders[:count]:
+            for work, n, step in filter(None, riders[:count]):
                 work(n, step)
                 if work == turn_back and (step + 1) % (PAIR * CB) == 0:
                     gain_bias_round(n * CHUNK_PAIRS + step // (PAIR * CB))
@@ -198,6 +198,7 @@ def tile_stoichiometricmab_kernel(tc, base, x, ln_gain, ln_bias, w1, b1, w2, b2,
             nc.vector.tensor_tensor(window[cb][:].indirect(offsets[:]), mlp[cb][:], x_sb[:, cb, :], ALU.add)
             nc.sync.dma_start(out[cb * P : (cb + 1) * P, :], window[cb][:])
 
+        free_places = [None] * STEPS
         chunk = [slice(n * TOK, (n + 1) * TOK) for n in range(NCH)]
         last_pairs = [slice(N - 2 * PAIR * P, N - PAIR * P), slice(N - PAIR * P, N)]
         ride(turning(0), STEPS)
@@ -208,10 +209,10 @@ def tile_stoichiometricmab_kernel(tc, base, x, ln_gain, ln_bias, w1, b1, w2, b2,
         first_matmul(chunk[0], turning(2) + turning_back(1), split=2)
         second_matmul(chunk[0], 0)
         normalise(2)
-        first_matmul(chunk[1], turning(3) + turning_back(2))
+        first_matmul(chunk[1], turning_back(2) + turning(3))
         second_matmul(chunk[1], 0)
         normalise(3)
-        first_matmul(chunk[2], turning_back(3))
+        first_matmul(chunk[2], free_places + turning_back(3))
         second_matmul(chunk[2], 0)
         for pair in last_pairs:
             first_matmul(pair, [])

@@ -53,7 +53,8 @@ def tile_stoichiometricmab_kernel(tc, base, x, ln_gain, ln_bias, w1, b1, w2, b2,
             nc.sync.dma_start(columns[:], vector.rearrange("(r p) o -> p (r o)", p=P))
             return columns
 
-        load_x(0, TOK // 2)
+        for t in range(PAIR):
+            load_x(t * P, P)
         load_x(TOK // 2, TOK // 2)
         load_x(TOK, TOK)
         gain_col = load_columns(ln_gain, CB, "gain_col")
@@ -80,15 +81,18 @@ def tile_stoichiometricmab_kernel(tc, base, x, ln_gain, ln_bias, w1, b1, w2, b2,
         rstd = held.tile([P, NT], F32, name="rstd")
         x_hat = held.tile([P, NT, C], F32, name="x_hat")
         nrm = held.tile([P, CB, N], BF16, name="nrm")
+        turn_bank = [None]
         x_turned = {}
         turned_back = {}
 
         def turn(n, step):
             t, cb = n * TILES + step // CB, step % CB
             i, k = t // PAIR, t % PAIR
-            if k == 0 and cb == 0:
-                x_turned[i] = psum.tile([P, TOK], F32, name="x_turned", tag="bank")
-            nc.tensor.transpose(x_turned[i][:, k * C + cb * P : k * C + (cb + 1) * P], x_sb[:, cb, t * P : (t + 1) * P], ident[:])
+            if cb == 0:
+                if n == 0 or k == 0:
+                    turn_bank[0] = psum.tile([P, TOK], F32, name="x_turned", tag="bank")
+                x_turned[t] = turn_bank[0][:, k * C : (k + 1) * C]
+            nc.tensor.transpose(x_turned[t][:, cb * P : (cb + 1) * P], x_sb[:, cb, t * P : (t + 1) * P], ident[:])
 
         def normalise(n):
             tiles = range(n * TILES, (n + 1) * TILES)
@@ -105,14 +109,14 @@ def tile_stoichiometricmab_kernel(tc, base, x, ln_gain, ln_bias, w1, b1, w2, b2,
                         nc.gpsimd.tensor_tensor(rstd[:, pair], var_eps[:, pair], minus_half[:], ALU.pow)
 
             for t in tiles:
-                nc.vector.bn_stats(stats[:, t, :], x_turned[t // PAIR][:, (t % PAIR) * C : (t % PAIR + 1) * C])
+                nc.vector.bn_stats(stats[:, t, :], x_turned[t])
                 if t > tiles[0]:
                     aggregate(t - 1)
             aggregate(tiles[-1])
             for t in tiles:
                 nc.vector.tensor_scalar(
                     x_hat[:, t, :],
-                    x_turned[t // PAIR][:, (t % PAIR) * C : (t % PAIR + 1) * C],
+                    x_turned[t],
                     mean_var[:, t, 0:1],
                     rstd[:, t : t + 1],
                     ALU.subtract,
@@ -209,7 +213,7 @@ def tile_stoichiometricmab_kernel(tc, base, x, ln_gain, ln_bias, w1, b1, w2, b2,
         first_matmul(chunk[0], turning(2) + turning_back(1), split=2)
         second_matmul(chunk[0], 0)
         normalise(2)
-        first_matmul(chunk[1], turning_back(2) + turning(3))
+        first_matmul(chunk[1], free_places[:4] + turning_back(2) + turning(3))
         second_matmul(chunk[1], 0)
         normalise(3)
         first_matmul(chunk[2], free_places + turning_back(3))

@@ -53,9 +53,8 @@ def tile_stoichiometricmab_kernel(tc, base, x, ln_gain, ln_bias, w1, b1, w2, b2,
             nc.sync.dma_start(columns[:], vector.rearrange("(r p) o -> p (r o)", p=P))
             return columns
 
-        for t in range(PAIR):
+        for t in range(TILES):
             load_x(t * P, P)
-        load_x(TOK // 2, TOK // 2)
         load_x(TOK, TOK)
         gain_col = load_columns(ln_gain, CB, "gain_col")
         bias_col = load_columns(ln_bias, CB, "bias_col")

import concourse.mybir as mybir
from concourse.masks import make_identity

F32 = mybir.dt.float32
BF16 = mybir.dt.bfloat16
U16 = mybir.dt.uint16
ALU = mybir.AluOpType
ACT = mybir.ActivationFunctionType

P = 128
C, F, S, N = 256, 1024, 4096, 2048
CB = C // P
FB = F // P
TOK = 512
NCH = N // TOK
NT = N // P
PAIR = TOK // C
TILES = TOK // P
CHUNK_PAIRS = TILES // PAIR
STEPS = TILES * CB
assert FB * CB == 2 * STEPS
EPS = 1e-5

FLOPS = 2 * N * C * F * 2


def tile_stoichiometricmab_kernel(tc, base, x, ln_gain, ln_bias, w1, b1, w2, b2, offs, out):
    nc = tc.nc
    with (
        tc.tile_pool(name="held", bufs=1) as held,
        tc.psum_pool(name="psum", bufs=8) as psum,
    ):
        ident = held.tile([P, P], F32, name="ident")
        make_identity(nc, ident[:])
        minus_half = held.tile([P, PAIR], F32, name="minus_half")
        nc.vector.memset(minus_half[:], -0.5)
        eps_col = held.tile([P, 1], F32, name="eps_col")
        nc.vector.memset(eps_col[:], EPS)
        one = held.tile([P, 1], F32, name="one")
        nc.vector.memset(one[:], 1.0)
        table_warm = held.tile([P, 2], F32, name="table_warm")
        nc.scalar.activation(table_warm[:, 0:1], one[:], ACT.Abs_reciprocal_sqrt)

        x_sb = held.tile([P, CB, N], F32, name="x_sb")
        x_blocks = x.rearrange("(cb p) n -> p cb n", p=P)

        def load_x(first_token, tokens):
            part = slice(first_token, first_token + tokens)
            nc.sync.dma_start(x_sb[:, :, part], x_blocks[:, :, part])

        def load_columns(vector, blocks, name):
            columns = held.tile([P, blocks], F32, name=name)
            nc.sync.dma_start(columns[:], vector.rearrange("(r p) o -> p (r o)", p=P))
            return columns

        for t in range(TILES):
            load_x(t * P, P)
        load_x(TOK, TOK)
        gain_col = load_columns(ln_gain, CB, "gain_col")
        bias_col = load_columns(ln_bias, CB, "bias_col")
        w1_sb = held.tile([P, CB, F], BF16, name="w1_sb")
        nc.sync.dma_start(w1_sb[:], w1.rearrange("(cb p) f -> p cb f", p=P))
        b1_col = load_columns(b1, FB, "b1_col")
        load_x(2 * TOK, TOK)
        load_x(3 * TOK, TOK)
        w2_sb = held.tile([P, FB, C], BF16, name="w2_sb")
        nc.sync.dma_start(w2_sb[:], w2.rearrange("(fb p) c -> p fb c", p=P))
        b2_col = load_columns(b2, CB, "b2_col")

        offsets = held.tile([P, N // 16], U16, name="offsets")
        nc.sync.dma_start(offsets[:], offs)

        window = [held.tile([P, S], F32, name=f"window{cb}") for cb in range(CB)]
        for cb in range(CB):
            nc.sync.dma_start(window[cb][:], base[cb * P : (cb + 1) * P, :])

        stats = held.tile([P, NT, 6], F32, name="stats")
        mean_var = held.tile([P, NT, 2], F32, name="mean_var")
        var_eps = held.tile([P, NT], F32, name="var_eps")
        rstd = held.tile([P, NT], F32, name="rstd")
        x_hat = held.tile([P, NT, C], F32, name="x_hat")
        nrm = held.tile([P, CB, N], BF16, name="nrm")
        turn_bank = [None]
        x_turned = {}
        turned_back = {}

        def turn(n, step):
            t, cb = n * TILES + step // CB, step % CB
            i, k = t // PAIR, t % PAIR
            if cb == 0:
                if n == 0 or k == 0:
                    turn_bank[0] = psum.tile([P, TOK], F32, name="x_turned", tag="bank")
                x_turned[t] = turn_bank[0][:, k * C : (k + 1) * C]
            nc.tensor.transpose(x_turned[t][:, cb * P : (cb + 1) * P], x_sb[:, cb, t * P : (t + 1) * P], ident[:])

        def normalise(n):
            tiles = range(n * TILES, (n + 1) * TILES)
            def aggregate(t):
                nc.vector.bn_aggr(mean_var[:, t, :], stats[:, t, :])
                if t % PAIR == PAIR - 1:
                    pair = slice(t + 1 - PAIR, t + 1)
                    if n == 0:
                        nc.scalar.activation(rstd[:, pair], mean_var[:, pair, 1], ACT.Abs_reciprocal_sqrt, bias=eps_col[:])
                        if t == tiles[-1]:
                            nc.scalar.activation(table_warm[:, 1:2], rstd[:, t : t + 1], ACT.Gelu)
                    else:
                        nc.vector.tensor_scalar_add(var_eps[:, pair], mean_var[:, pair, 1], EPS)
                        nc.gpsimd.tensor_tensor(rstd[:, pair], var_eps[:, pair], minus_half[:], ALU.pow)

            for t in tiles:
                nc.vector.bn_stats(stats[:, t, :], x_turned[t])
                if t > tiles[0]:
                    aggregate(t - 1)
            aggregate(tiles[-1])
            for t in tiles:
                nc.vector.tensor_scalar(
                    x_hat[:, t, :],
                    x_turned[t],
                    mean_var[:, t, 0:1],
                    rstd[:, t : t + 1],
                    ALU.subtract,
                    ALU.mult,
                )

        def turn_back(n, step):
            t, cb = n * TILES + step // CB, step % CB
            i, k = t // PAIR, t % PAIR
            if k == 0 and cb == 0:
                turned_back[i] = psum.tile([P, CB, PAIR * P], F32, name="turned_back", tag="bank")
            nc.tensor.transpose(turned_back[i][:, cb, k * P : (k + 1) * P], x_hat[:, t, cb * P : (cb + 1) * P], ident[:])

        def gain_bias_round(i):
            for cb in range(CB):
                part = slice(i * PAIR * P, (i + 1) * PAIR * P)
                if i == 0 or i >= 2 * CHUNK_PAIRS:
                    nc.vector.tensor_scalar(
                        nrm[:, cb, part], turned_back[i][:, cb, :], gain_col[:, cb : cb + 1], bias_col[:, cb : cb + 1], ALU.mult, ALU.add
                    )
                else:
                    nc.scalar.activation(
                        nrm[:, cb, part], turned_back[i][:, cb, :], ACT.Identity, bias=bias_col[:, cb : cb + 1], scale=gain_col[:, cb : cb + 1]
                    )

        def turning(n):
            return [(turn, n, step) for step in range(STEPS)]

        def turning_back(n):
            return [(turn_back, n, step) for step in range(STEPS)]

        def ride(riders, count):
            for work, n, step in filter(None, riders[:count]):
                work(n, step)
                if work == turn_back and (step + 1) % (PAIR * CB) == 0:
                    gain_bias_round(n * CHUNK_PAIRS + step // (PAIR * CB))
            riders[:count] = []

        hidden = held.tile([P, FB, N], BF16, name="hidden")
        mlp = [held.tile([P, N], F32, name=f"mlp{cb}") for cb in range(CB)]

        def first_matmul(tokens, riders, split=0):
            h_ps = {}
            width = tokens.stop - tokens.start

            def multiply(fb, part):
                for cb in range(CB):
                    nc.tensor.matmul(
                        h_ps[fb][:, part.start - tokens.start : part.stop - tokens.start],
                        w1_sb[:, cb, fb * P : (fb + 1) * P],
                        nrm[:, cb, part],
                        start=(cb == 0),
                        stop=(cb == CB - 1),
                    )
                    if part == tokens:
                        matmuls_left = (FB - fb) * CB - cb
                        ride(riders, 2 if len(riders) >= 2 * matmuls_left else 1)

            middle = tokens.start + PAIR * P
            for fb in range(split):
                h_ps[fb] = psum.tile([P, width], F32, name="h_ps", tag="bank")
                multiply(fb, slice(tokens.start, middle))
            for fb in range(FB):
                if fb < split:
                    multiply(fb, slice(middle, tokens.stop))
                else:
                    h_ps[fb] = psum.tile([P, width], F32, name="h_ps", tag="bank")
                    multiply(fb, tokens)
                nc.scalar.activation(hidden[:, fb, tokens], h_ps[fb][:], ACT.Gelu, bias=b1_col[:, fb : fb + 1])

        def second_matmul(tokens, cb):
            mlp_ps = psum.tile([P, tokens.stop - tokens.start], F32, name="mlp_ps", tag="bank")
            for fb in range(FB):
                nc.tensor.matmul(
                    mlp_ps[:], w2_sb[:, fb, cb * P : (cb + 1) * P], hidden[:, fb, tokens], start=(fb == 0), stop=(fb == FB - 1)
                )
            if cb == 0:
                nc.vector.tensor_scalar_add(mlp[cb][:, tokens], mlp_ps[:], b2_col[:, cb : cb + 1])
            else:
                nc.scalar.activation(mlp[cb][:, tokens], mlp_ps[:], ACT.Identity, bias=b2_col[:, cb : cb + 1])

        def place(cb):
            nc.vector.tensor_tensor(window[cb][:].indirect(offsets[:]), mlp[cb][:], x_sb[:, cb, :], ALU.add)
            nc.sync.dma_start(out[cb * P : (cb + 1) * P, :], window[cb][:])

        free_places = [None] * STEPS
        chunk = [slice(n * TOK, (n + 1) * TOK) for n in range(NCH)]
        last_pairs = [slice(N - 2 * PAIR * P, N - PAIR * P), slice(N - PAIR * P, N)]
        ride(turning(0), STEPS)
        normalise(0)
        ride(turning(1), STEPS)
        ride(turning_back(0), STEPS)
        normalise(1)
        first_matmul(chunk[0], turning(2) + turning_back(1), split=2)
        second_matmul(chunk[0], 0)
        normalise(2)
        first_matmul(chunk[1], free_places[:4] + turning_back(2) + turning(3))
        second_matmul(chunk[1], 0)
        normalise(3)
        first_matmul(chunk[2], free_places + turning_back(3))
        second_matmul(chunk[2], 0)
        for pair in last_pairs:
            first_matmul(pair, [])
        for pair in last_pairs:
            second_matmul(pair, 0)
        place(0)
        for n in range(NCH):
            second_matmul(chunk[n], 1)
        place(1)
